import numpy as np
import ml_dtypes

BF16 = ml_dtypes.bfloat16


def bf(x):
    return np.asarray(x, np.float32).astype(BF16)


def f32(x):
    return np.asarray(x, np.float32)


def f64(x):
    return np.asarray(x).astype(np.float64)


def striped(idx):
    return np.tile(idx.reshape(-1, 16).T, (8, 1))


C, S, N, B, T, NH, DH = 512, 1024, 2048, 4, 512, 4, 128


def setup_inputs():
    r = np.random.standard_normal
    return {
        'tok_emb': f32(r((C, S))),
        'pos_emb': f32(r((C, T))),
        'wq': bf(r((C, C)) / np.sqrt(C)),
        'bq': f32(0.1 * r((C, 1))),
        'wk': bf(r((C, C)) / np.sqrt(C)),
        'wv': bf(r((C, C)) / np.sqrt(C)),
        'bv': f32(0.1 * r((C, 1))),
        'wo': bf(r((C, C)) / np.sqrt(C)),
        'bo': f32(0.1 * r((C, 1))),
        'offs': striped(np.concatenate([np.random.permutation(S)[:T] for _ in range(B)])),
    }


def heads(a):
    return a.reshape(NH, DH, B, T).transpose(2, 0, 1, 3)


def reference(tok_emb, pos_emb, wq, bq, wk, wv, bv, wo, bo, offs):
    idx = offs[:16].T.reshape(-1)
    x = f64(tok_emb)[:, idx] + np.tile(f64(pos_emb), (1, B))
    q = heads(f64(wq).T @ x + f64(bq))
    k = heads(f64(wk).T @ x)
    v = heads(f64(wv).T @ x + f64(bv))
    sc = (q.transpose(0, 1, 3, 2) @ k) / np.sqrt(DH)
    keep = np.arange(T)[:, None] >= np.arange(T)[None, :]
    sc = np.where(keep, sc, -1e9)
    e = np.exp(sc - sc.max(axis=-1, keepdims=True))
    a = e / e.sum(axis=-1, keepdims=True)
    o = (v @ a.transpose(0, 1, 3, 2)).transpose(1, 2, 0, 3).reshape(C, N)
    return x + f64(wo).T @ o + f64(bo)

@@ -1,0 +1,166 @@
+import math
+
+import concourse.mybir as mybir
+from concourse.masks import make_identity
+
+F32 = mybir.dt.float32
+BF16 = mybir.dt.bfloat16
+U16 = mybir.dt.uint16
+ADD = mybir.AluOpType.add
+MULT = mybir.AluOpType.mult
+IS_GE = mybir.AluOpType.is_ge
+EXP = mybir.ActivationFunctionType.Exp
+IDENTITY = mybir.ActivationFunctionType.Identity
+X_AXIS = mybir.AxisListType.X
+
+P = 128
+C = 512
+S = 1024
+T = 512
+B = 4
+N = B * T
+CB = C // P
+TB = T // P
+SCALE = 1.0 / math.sqrt(P)
+MASKED = -1.0e10
+
+FLOPS = 4 * 2 * C * C * N + B * CB * 2 * 2 * P * (T * (T + 1) // 2)
+
+AT_WIDTH = [T - kb * P for kb in range(TB)]
+AT_START = [sum(AT_WIDTH[:kb]) for kb in range(TB)]
+AT_COLS = sum(AT_WIDTH)
+AT_SPLIT = AT_START[2]
+
+
+def tile_main_b_kernel(tc, tok_emb, pos_emb, wq, bq, wk, wv, bv, wo, bo, offs, out):
+    nc = tc.nc
+    with (
+        tc.tile_pool(name="held", bufs=1) as held,
+        tc.tile_pool(name="seq", bufs=2) as seq,
+        tc.tile_pool(name="head", bufs=2) as head,
+        tc.tile_pool(name="stage", bufs=3) as stage,
+        tc.psum_pool(name="ps_proj", bufs=2) as ps_proj,
+        tc.psum_pool(name="ps_score", bufs=3) as ps_score,
+        tc.psum_pool(name="ps_at", bufs=1) as ps_at,
+        tc.psum_pool(name="ps_o", bufs=1) as ps_o,
+    ):
+        offsets = held.tile([P, N // 16], U16, name="offsets")
+        nc.sync.dma_start(offsets[:], offs)
+        tok = [held.tile([P, S], F32, name=f"tok{cb}") for cb in range(CB)]
+        pos = [held.tile([P, T], F32, name=f"pos{cb}") for cb in range(CB)]
+        for cb in range(CB):
+            nc.sync.dma_start(tok[cb][:], tok_emb[cb * P : (cb + 1) * P, :])
+            nc.scalar.dma_start(pos[cb][:], pos_emb[cb * P : (cb + 1) * P, :])
+        wq_sb = held.tile([P, CB, C], BF16, name="wq_sb")
+        wk_sb = held.tile([P, CB, C], BF16, name="wk_sb")
+        wv_sb = held.tile([P, CB, C], BF16, name="wv_sb")
+        wo_sb = held.tile([P, CB, C], BF16, name="wo_sb")
+        for w_sb, w in ((wq_sb, wq), (wk_sb, wk), (wv_sb, wv), (wo_sb, wo)):
+            nc.gpsimd.dma_start(w_sb[:], w.rearrange("(cb p) m -> p cb m", p=P))
+        bq_sb = held.tile([P, CB], F32, name="bq_sb")
+        bv_sb = held.tile([P, CB], F32, name="bv_sb")
+        bo_sb = held.tile([P, CB], F32, name="bo_sb")
+        with nc.allow_non_contiguous_dma(reason="one bias value to a partition"):
+            for b_sb, b in ((bq_sb, bq), (bv_sb, bv), (bo_sb, bo)):
+                nc.scalar.dma_start(b_sb[:], b.rearrange("(a p) o -> p (a o)", p=P))
+
+        ident = held.tile([P, P], BF16, name="ident")
+        make_identity(nc, ident[:])
+        causal = held.tile([P, P], BF16, name="causal")
+        nc.gpsimd.memset(causal[:], 0.0)
+        nc.gpsimd.affine_select(
+            out=causal[:], in_=causal[:], pattern=[[-1, P]], compare_op=IS_GE,
+            fill=MASKED, base=0, channel_multiplier=1,
+        )
+        bq_scaled = held.tile([P, CB], F32, name="bq_scaled")
+        nc.vector.tensor_scalar(out=bq_scaled[:], in0=bq_sb[:], scalar1=SCALE, scalar2=None, op0=MULT)
+
+        def embed(r):
+            x32 = seq.tile([P, CB, T], F32, name="x32")
+            xbf = seq.tile([P, CB, T], BF16, name="xbf")
+            piece = offsets[:, r * (T // 16) : (r + 1) * (T // 16)]
+            for cb in range(CB):
+                nc.vector.tensor_tensor(x32[:, cb, :], tok[cb][:].indirect(piece), pos[cb][:], ADD)
+                nc.gpsimd.tensor_scalar(out=xbf[:, cb, :], in0=x32[:, cb, :], scalar1=1.0, scalar2=None, op0=MULT)
+            return x32, xbf
+
+        def project(xbf):
+            q = seq.tile([P, CB, T], BF16, name="q")
+            k = seq.tile([P, CB, T], BF16, name="k")
+            v_t = seq.tile([P, TB, C], BF16, name="v_t")
+            for h in range(CB):
+                acc_q = ps_proj.tile([P, T], F32, name="acc")
+                for cb in range(CB):
+                    nc.tensor.matmul(acc_q[:], wq_sb[:, cb, h * P : (h + 1) * P], xbf[:, cb, :],
+                                     start=(cb == 0), stop=(cb == CB - 1))
+                nc.scalar.activation(q[:, h, :], acc_q[:], IDENTITY, bias=bq_scaled[:, h : h + 1], scale=SCALE)
+                acc_k = ps_proj.tile([P, T], F32, name="acc")
+                for cb in range(CB):
+                    nc.tensor.matmul(acc_k[:], wk_sb[:, cb, h * P : (h + 1) * P], xbf[:, cb, :],
+                                     start=(cb == 0), stop=(cb == CB - 1))
+                nc.vector.tensor_copy(k[:, h, :], acc_k[:])
+            for tb in range(TB):
+                acc_v = ps_proj.tile([P, C], F32, name="acc")
+                for cb in range(CB):
+                    nc.tensor.matmul(acc_v[:], xbf[:, cb, tb * P : (tb + 1) * P], wv_sb[:, cb, :],
+                                     start=(cb == 0), stop=(cb == CB - 1))
+                nc.scalar.copy(v_t[:, tb, :], acc_v[:])
+            return q, k, v_t
+
+        def attend(q, k, v_t, o, h):
+            neg_max = head.tile([P, TB], F32, name="neg_max")
+            row_sum = head.tile([P, TB], F32, name="row_sum")
+            e = head.tile([P, TB, T], BF16, name="e")
+            for tb in range(TB):
+                width = (tb + 1) * P
+                score = ps_score.tile([P, T], F32, name="score")
+                nc.tensor.matmul(score[:, :width], q[:, h, tb * P : (tb + 1) * P], k[:, h, :width],
+                                 start=True, stop=False)
+                nc.tensor.matmul(score[:, tb * P : width], ident[:], causal[:], start=False, stop=True)
+                nc.vector.reduce_max(neg_max[:, tb : tb + 1], score[:, :width], X_AXIS, negate=True)
+                nc.scalar.activation(e[:, tb, :width], score[:, :width], EXP, bias=neg_max[:, tb : tb + 1],
+                                     scale=1.0, accum_out=row_sum[:, tb : tb + 1])
+            inv_sum = head.tile([P, TB], F32, name="inv_sum")
+            nc.vector.reciprocal(inv_sum[:], row_sum[:])
+            diag = head.tile([P, TB, P], BF16, name="diag")
+            at_lo = ps_at.tile([P, AT_SPLIT], BF16, name="at_lo")
+            at_hi = ps_at.tile([P, AT_COLS - AT_SPLIT], BF16, name="at_hi")
+            for tb in range(TB):
+                nc.gpsimd.tensor_scalar(out=diag[:, tb, :], in0=ident[:], scalar1=inv_sum[:, tb : tb + 1],
+                                        scalar2=None, op0=MULT)
+                for kb in range(tb + 1):
+                    col = AT_START[kb] + (tb - kb) * P
+                    bank, col = (at_lo, col) if col < AT_SPLIT else (at_hi, col - AT_SPLIT)
+                    nc.tensor.matmul(bank[:, col : col + P], e[:, tb, kb * P : (kb + 1) * P], diag[:, tb, :],
+                                     start=True, stop=True)
+            a_t = head.tile([P, AT_COLS], BF16, name="a_t")
+            nc.vector.tensor_copy(a_t[:, :AT_SPLIT], at_lo[:])
+            nc.vector.tensor_copy(a_t[:, AT_SPLIT:], at_hi[:])
+            o_acc = ps_o.tile([P, T], F32, name="o_acc")
+            for kb in range(TB):
+                nc.tensor.matmul(o_acc[:, kb * P :], v_t[:, kb, h * P : (h + 1) * P],
+                                 a_t[:, AT_START[kb] : AT_START[kb] + AT_WIDTH[kb]],
+                                 start=(kb == 0), stop=(kb == TB - 1))
+            nc.scalar.activation(o[:, h, :], o_acc[:], IDENTITY, bias=bv_sb[:, h : h + 1], scale=1.0)
+
+        def finish(r, x32, o):
+            for mb in range(CB):
+                acc_out = ps_proj.tile([P, T], F32, name="acc")
+                for cb in range(CB):
+                    nc.tensor.matmul(acc_out[:], wo_sb[:, cb, mb * P : (mb + 1) * P], o[:, cb, :],
+                                     start=(cb == 0), stop=(cb == CB - 1))
+                res = stage.tile([P, T], F32, name="res")
+                nc.vector.scalar_tensor_tensor(out=res[:], in0=acc_out[:], scalar=bo_sb[:, mb : mb + 1],
+                                               in1=x32[:, mb, :], op0=ADD, op1=ADD)
+                nc.sync.dma_start(out[mb * P : (mb + 1) * P, r * T : (r + 1) * T], res[:])
+
+        embedded = embed(0)
+        for r in range(B):
+            x32, xbf = embedded
+            q, k, v_t = project(xbf)
+            if r + 1 < B:
+                embedded = embed(r + 1)
+            o = seq.tile([P, CB, T], BF16, name="o")
+            for h in range(CB):
+                attend(q, k, v_t, o, h)
+            finish(r, x32, o)

@@ -36,33 +36,34 @@ def tile_main_b_kernel(tc, tok_emb, pos_emb, wq, bq, wk, wv, bv, wo, bo, offs, o
     nc = tc.nc
     with (
         tc.tile_pool(name="held", bufs=1) as held,
-        tc.tile_pool(name="seq", bufs=2) as seq,
         tc.tile_pool(name="head", bufs=2) as head,
         tc.tile_pool(name="stage", bufs=3) as stage,
-        tc.psum_pool(name="ps_proj", bufs=2) as ps_proj,
-        tc.psum_pool(name="ps_score", bufs=3) as ps_score,
-        tc.psum_pool(name="ps_at", bufs=1) as ps_at,
-        tc.psum_pool(name="ps_o", bufs=1) as ps_o,
+        tc.psum_pool(name="psum", bufs=8) as psum,
     ):
         offsets = held.tile([P, N // 16], U16, name="offsets")
         nc.sync.dma_start(offsets[:], offs)
         tok = [held.tile([P, S], F32, name=f"tok{cb}") for cb in range(CB)]
         pos = [held.tile([P, T], F32, name=f"pos{cb}") for cb in range(CB)]
-        for cb in range(CB):
-            nc.sync.dma_start(tok[cb][:], tok_emb[cb * P : (cb + 1) * P, :])
-            nc.scalar.dma_start(pos[cb][:], pos_emb[cb * P : (cb + 1) * P, :])
         wq_sb = held.tile([P, CB, C], BF16, name="wq_sb")
         wk_sb = held.tile([P, CB, C], BF16, name="wk_sb")
         wv_sb = held.tile([P, CB, C], BF16, name="wv_sb")
         wo_sb = held.tile([P, CB, C], BF16, name="wo_sb")
-        for w_sb, w in ((wq_sb, wq), (wk_sb, wk), (wv_sb, wv), (wo_sb, wo)):
-            nc.gpsimd.dma_start(w_sb[:], w.rearrange("(cb p) m -> p cb m", p=P))
         bq_sb = held.tile([P, CB], F32, name="bq_sb")
         bv_sb = held.tile([P, CB], F32, name="bv_sb")
         bo_sb = held.tile([P, CB], F32, name="bo_sb")
+        for cb in range(CB):
+            rows = slice(cb * P, (cb + 1) * P)
+            nc.sync.dma_start(tok[cb][:], tok_emb[rows, :])
+            nc.scalar.dma_start(pos[cb][:], pos_emb[rows, :])
+            nc.sync.dma_start(wq_sb[:, cb, :], wq[rows, :])
+            nc.scalar.dma_start(wk_sb[:, cb, :], wk[rows, :])
         with nc.allow_non_contiguous_dma(reason="one bias value to a partition"):
-            for b_sb, b in ((bq_sb, bq), (bv_sb, bv), (bo_sb, bo)):
-                nc.scalar.dma_start(b_sb[:], b.rearrange("(a p) o -> p (a o)", p=P))
+            nc.sync.dma_start(bq_sb[:], bq.rearrange("(a p) o -> p (a o)", p=P))
+        nc.sync.dma_start(wv_sb[:], wv.rearrange("(cb p) m -> p cb m", p=P))
+        nc.sync.dma_start(wo_sb[:], wo.rearrange("(cb p) m -> p cb m", p=P))
+        with nc.allow_non_contiguous_dma(reason="one bias value to a partition"):
+            nc.sync.dma_start(bv_sb[:], bv.rearrange("(a p) o -> p (a o)", p=P))
+            nc.sync.dma_start(bo_sb[:], bo.rearrange("(a p) o -> p (a o)", p=P))
 
         ident = held.tile([P, P], BF16, name="ident")
         make_identity(nc, ident[:])
@@ -72,95 +73,151 @@ def tile_main_b_kernel(tc, tok_emb, pos_emb, wq, bq, wk, wv, bv, wo, bo, offs, o
             out=causal[:], in_=causal[:], pattern=[[-1, P]], compare_op=IS_GE,
             fill=MASKED, base=0, channel_multiplier=1,
         )
-        bq_scaled = held.tile([P, CB], F32, name="bq_scaled")
-        nc.vector.tensor_scalar(out=bq_scaled[:], in0=bq_sb[:], scalar1=SCALE, scalar2=None, op0=MULT)
 
-        def embed(r):
-            x32 = seq.tile([P, CB, T], F32, name="x32")
-            xbf = seq.tile([P, CB, T], BF16, name="xbf")
+        x32 = held.tile([P, CB, N], F32, name="x32")
+        xbf = held.tile([P, CB, N], BF16, name="xbf")
+        q = held.tile([P, CB, N], BF16, name="q")
+        k = held.tile([P, CB, N], BF16, name="k")
+        v_t = held.tile([P, B * TB, C], BF16, name="v_t")
+        o = held.tile([P, CB, N], BF16, name="o")
+
+        def bank(name, columns=T, dtype=F32):
+            return psum.tile([P, columns], dtype, name=name, tag="bank")
+
+        def embed(r, cb):
+            cols = slice(r * T, (r + 1) * T)
             piece = offsets[:, r * (T // 16) : (r + 1) * (T // 16)]
+            nc.vector.tensor_tensor(x32[:, cb, cols], tok[cb][:].indirect(piece), pos[cb][:], ADD)
+            nc.scalar.copy(xbf[:, cb, cols], x32[:, cb, cols])
+
+        def q_part(acc, r, h, cb):
+            nc.tensor.matmul(acc[:], wq_sb[:, cb, h * P : (h + 1) * P], xbf[:, cb, r * T : (r + 1) * T],
+                             start=(cb == 0), stop=(cb == CB - 1))
+
+        def q_store(acc, r, h):
+            nc.scalar.activation(q[:, h, r * T : (r + 1) * T], acc[:], IDENTITY, bias=bq_sb[:, h : h + 1], scale=1.0)
+
+        def k_part(acc, r, h, cb):
+            nc.tensor.matmul(acc[:], wk_sb[:, cb, h * P : (h + 1) * P], xbf[:, cb, r * T : (r + 1) * T],
+                             start=(cb == 0), stop=(cb == CB - 1))
+
+        def k_store(acc, r, h):
+            nc.vector.tensor_scalar(out=k[:, h, r * T : (r + 1) * T], in0=acc[:], scalar1=SCALE, scalar2=None, op0=MULT)
+
+        def v_part(acc, r, tb, cb):
+            first = r * T + tb * P
+            nc.tensor.matmul(acc[:], xbf[:, cb, first : first + P], wv_sb[:, cb, :],
+                             start=(cb == 0), stop=(cb == CB - 1))
+
+        def v_store(acc, r, tb):
+            nc.scalar.copy(v_t[:, r * TB + tb, :], acc[:])
+
+        def out_part(acc, r, mb, cb):
+            nc.tensor.matmul(acc[:], wo_sb[:, cb, mb * P : (mb + 1) * P], o[:, cb, r * T : (r + 1) * T],
+                             start=(cb == 0), stop=(cb == CB - 1))
+
+        def out_store(acc, r, mb):
+            res = stage.tile([P, T], F32, name="res")
+            nc.vector.scalar_tensor_tensor(out=res[:], in0=acc[:], scalar=bo_sb[:, mb : mb + 1],
+                                           in1=x32[:, mb, r * T : (r + 1) * T], op0=ADD, op1=ADD)
+            nc.sync.dma_start(out[mb * P : (mb + 1) * P, r * T : (r + 1) * T], res[:])
+
+        def project(part, store, r, i):
+            acc = bank("acc")
             for cb in range(CB):
-                nc.vector.tensor_tensor(x32[:, cb, :], tok[cb][:].indirect(piece), pos[cb][:], ADD)
-                nc.gpsimd.tensor_scalar(out=xbf[:, cb, :], in0=x32[:, cb, :], scalar1=1.0, scalar2=None, op0=MULT)
-            return x32, xbf
+                part(acc, r, i, cb)
+            store(acc, r, i)
 
-        def project(xbf):
-            q = seq.tile([P, CB, T], BF16, name="q")
-            k = seq.tile([P, CB, T], BF16, name="k")
-            v_t = seq.tile([P, TB, C], BF16, name="v_t")
-            for h in range(CB):
-                acc_q = ps_proj.tile([P, T], F32, name="acc")
-                for cb in range(CB):
-                    nc.tensor.matmul(acc_q[:], wq_sb[:, cb, h * P : (h + 1) * P], xbf[:, cb, :],
-                                     start=(cb == 0), stop=(cb == CB - 1))
-                nc.scalar.activation(q[:, h, :], acc_q[:], IDENTITY, bias=bq_scaled[:, h : h + 1], scale=SCALE)
-                acc_k = ps_proj.tile([P, T], F32, name="acc")
-                for cb in range(CB):
-                    nc.tensor.matmul(acc_k[:], wk_sb[:, cb, h * P : (h + 1) * P], xbf[:, cb, :],
-                                     start=(cb == 0), stop=(cb == CB - 1))
-                nc.vector.tensor_copy(k[:, h, :], acc_k[:])
-            for tb in range(TB):
-                acc_v = ps_proj.tile([P, C], F32, name="acc")
-                for cb in range(CB):
-                    nc.tensor.matmul(acc_v[:], xbf[:, cb, tb * P : (tb + 1) * P], wv_sb[:, cb, :],
-                                     start=(cb == 0), stop=(cb == CB - 1))
-                nc.scalar.copy(v_t[:, tb, :], acc_v[:])
-            return q, k, v_t
+        def new_head():
+            return {
+                "neg_max": head.tile([P, TB], F32, name="neg_max"),
+                "row_sum": head.tile([P, TB], F32, name="row_sum"),
+                "inv_sum": head.tile([P, TB], F32, name="inv_sum"),
+                "e": head.tile([P, TB, T], BF16, name="e"),
+                "diag": head.tile([P, TB, P], BF16, name="diag"),
+            }
 
-        def attend(q, k, v_t, o, h):
-            neg_max = head.tile([P, TB], F32, name="neg_max")
-            row_sum = head.tile([P, TB], F32, name="row_sum")
-            e = head.tile([P, TB, T], BF16, name="e")
+        def score_block(r, h, tb, soft):
+            width = (tb + 1) * P
+            score = bank("score")
+            nc.tensor.matmul(score[:, :width], q[:, h, r * T + tb * P : r * T + width], k[:, h, r * T : r * T + width],
+                             start=True, stop=False)
+            nc.tensor.matmul(score[:, tb * P : width], ident[:], causal[:], start=False, stop=True)
+            nc.vector.reduce_max(soft["neg_max"][:, tb : tb + 1], score[:, :width], X_AXIS, negate=True)
+            nc.scalar.activation(soft["e"][:, tb, :width], score[:, :width], EXP, bias=soft["neg_max"][:, tb : tb + 1],
+                                 scale=1.0, accum_out=soft["row_sum"][:, tb : tb + 1])
+
+        def normalisers(soft):
+            nc.vector.reciprocal(soft["inv_sum"][:], soft["row_sum"][:])
             for tb in range(TB):
-                width = (tb + 1) * P
-                score = ps_score.tile([P, T], F32, name="score")
-                nc.tensor.matmul(score[:, :width], q[:, h, tb * P : (tb + 1) * P], k[:, h, :width],
-                                 start=True, stop=False)
-                nc.tensor.matmul(score[:, tb * P : width], ident[:], causal[:], start=False, stop=True)
-                nc.vector.reduce_max(neg_max[:, tb : tb + 1], score[:, :width], X_AXIS, negate=True)
-                nc.scalar.activation(e[:, tb, :width], score[:, :width], EXP, bias=neg_max[:, tb : tb + 1],
-                                     scale=1.0, accum_out=row_sum[:, tb : tb + 1])
-            inv_sum = head.tile([P, TB], F32, name="inv_sum")
-            nc.vector.reciprocal(inv_sum[:], row_sum[:])
-            diag = head.tile([P, TB, P], BF16, name="diag")
-            at_lo = ps_at.tile([P, AT_SPLIT], BF16, name="at_lo")
-            at_hi = ps_at.tile([P, AT_COLS - AT_SPLIT], BF16, name="at_hi")
-            for tb in range(TB):
-                nc.gpsimd.tensor_scalar(out=diag[:, tb, :], in0=ident[:], scalar1=inv_sum[:, tb : tb + 1],
+                nc.vector.tensor_scalar(out=soft["diag"][:, tb, :], in0=ident[:], scalar1=soft["inv_sum"][:, tb : tb + 1],
                                         scalar2=None, op0=MULT)
+
+        def transpose_weights(soft):
+            at_lo = bank("at_lo", AT_SPLIT, BF16)
+            at_hi = bank("at_hi", AT_COLS - AT_SPLIT, BF16)
+            for tb in range(TB):
                 for kb in range(tb + 1):
                     col = AT_START[kb] + (tb - kb) * P
-                    bank, col = (at_lo, col) if col < AT_SPLIT else (at_hi, col - AT_SPLIT)
-                    nc.tensor.matmul(bank[:, col : col + P], e[:, tb, kb * P : (kb + 1) * P], diag[:, tb, :],
-                                     start=True, stop=True)
+                    dest, col = (at_lo, col) if col < AT_SPLIT else (at_hi, col - AT_SPLIT)
+                    nc.tensor.matmul(dest[:, col : col + P], soft["e"][:, tb, kb * P : (kb + 1) * P],
+                                     soft["diag"][:, tb, :], start=True, stop=True)
             a_t = head.tile([P, AT_COLS], BF16, name="a_t")
             nc.vector.tensor_copy(a_t[:, :AT_SPLIT], at_lo[:])
             nc.vector.tensor_copy(a_t[:, AT_SPLIT:], at_hi[:])
-            o_acc = ps_o.tile([P, T], F32, name="o_acc")
+            return a_t
+
+        def weighted_sum(r, h, a_t):
+            o_acc = bank("o_acc")
             for kb in range(TB):
-                nc.tensor.matmul(o_acc[:, kb * P :], v_t[:, kb, h * P : (h + 1) * P],
+                nc.tensor.matmul(o_acc[:, kb * P :], v_t[:, r * TB + kb, h * P : (h + 1) * P],
                                  a_t[:, AT_START[kb] : AT_START[kb] + AT_WIDTH[kb]],
                                  start=(kb == 0), stop=(kb == TB - 1))
-            nc.scalar.activation(o[:, h, :], o_acc[:], IDENTITY, bias=bv_sb[:, h : h + 1], scale=1.0)
+            nc.scalar.activation(o[:, h, r * T : (r + 1) * T], o_acc[:], IDENTITY, bias=bv_sb[:, h : h + 1], scale=1.0)
 
-        def finish(r, x32, o):
-            for mb in range(CB):
-                acc_out = ps_proj.tile([P, T], F32, name="acc")
-                for cb in range(CB):
-                    nc.tensor.matmul(acc_out[:], wo_sb[:, cb, mb * P : (mb + 1) * P], o[:, cb, :],
-                                     start=(cb == 0), stop=(cb == CB - 1))
-                res = stage.tile([P, T], F32, name="res")
-                nc.vector.scalar_tensor_tensor(out=res[:], in0=acc_out[:], scalar=bo_sb[:, mb : mb + 1],
-                                               in1=x32[:, mb, :], op0=ADD, op1=ADD)
-                nc.sync.dma_start(out[mb * P : (mb + 1) * P, r * T : (r + 1) * T], res[:])
+        STEPS = B * CB
 
-        embedded = embed(0)
-        for r in range(B):
-            x32, xbf = embedded
-            q, k, v_t = project(xbf)
-            if r + 1 < B:
-                embedded = embed(r + 1)
-            o = seq.tile([P, CB, T], BF16, name="o")
+        accs_q = [bank(f"acc_q{h}") for h in range(CB)]
+        accs_k = [bank(f"acc_k{h}") for h in range(CB)]
+        for cb in range(CB):
+            embed(0, cb)
             for h in range(CB):
-                attend(q, k, v_t, o, h)
-            finish(r, x32, o)
+                q_part(accs_q[h], 0, h, cb)
+                k_part(accs_k[h], 0, h, cb)
+            embed(1, cb)
+        soft_next = new_head()
+        for h in range(CB):
+            q_store(accs_q[h], 0, h)
+            k_store(accs_k[h], 0, h)
+            if h == 1:
+                for tb in range(TB):
+                    score_block(0, 0, tb, soft_next)
+        for tb in range(TB):
+            project(v_part, v_store, 0, tb)
+        normalisers(soft_next)
+
+        for n in range(STEPS):
+            r, h = divmod(n, CB)
+            soft = soft_next
+            r1, h1 = divmod(n + 1, CB)
+            r2, h2 = divmod(n + 2, CB)
+            if n + 1 < STEPS:
+                soft_next = new_head()
+                for tb in range(TB):
+                    score_block(r1, h1, tb, soft_next)
+            if r + 2 < B:
+                embed(r + 2, h)
+            if CB <= n + 2 < STEPS:
+                project(q_part, q_store, r2, h2)
+            a_t = transpose_weights(soft)
+            if CB <= n + 2 < STEPS:
+                project(k_part, k_store, r2, h2)
+            if r + 1 < B:
+                project(v_part, v_store, r + 1, h)
+            weighted_sum(r, h, a_t)
+            if n + 1 < STEPS:
+                normalisers(soft_next)
+            if r >= 1:
+                project(out_part, out_store, r - 1, h)
+        for mb in range(CB):
+            project(out_part, out_store, B - 1, mb)

@@ -134,7 +134,6 @@ def tile_main_b_kernel(tc, tok_emb, pos_emb, wq, bq, wk, wv, bv, wo, bo, offs, o
                 "row_sum": head.tile([P, TB], F32, name="row_sum"),
                 "inv_sum": head.tile([P, TB], F32, name="inv_sum"),
                 "e": head.tile([P, TB, T], BF16, name="e"),
-                "diag": head.tile([P, TB, P], BF16, name="diag"),
             }
 
         def score_block(r, h, tb, soft):
@@ -150,8 +149,9 @@ def tile_main_b_kernel(tc, tok_emb, pos_emb, wq, bq, wk, wv, bv, wo, bo, offs, o
         def normalisers(soft):
             nc.vector.reciprocal(soft["inv_sum"][:], soft["row_sum"][:])
             for tb in range(TB):
-                nc.vector.tensor_scalar(out=soft["diag"][:, tb, :], in0=ident[:], scalar1=soft["inv_sum"][:, tb : tb + 1],
-                                        scalar2=None, op0=MULT)
+                width = (tb + 1) * P
+                nc.vector.tensor_scalar(out=soft["e"][:, tb, :width], in0=soft["e"][:, tb, :width],
+                                        scalar1=soft["inv_sum"][:, tb : tb + 1], scalar2=None, op0=MULT)
 
         def transpose_weights(soft):
             at_lo = bank("at_lo", AT_SPLIT, BF16)
@@ -160,8 +160,7 @@ def tile_main_b_kernel(tc, tok_emb, pos_emb, wq, bq, wk, wv, bv, wo, bo, offs, o
                 for kb in range(tb + 1):
                     col = AT_START[kb] + (tb - kb) * P
                     dest, col = (at_lo, col) if col < AT_SPLIT else (at_hi, col - AT_SPLIT)
-                    nc.tensor.matmul(dest[:, col : col + P], soft["e"][:, tb, kb * P : (kb + 1) * P],
-                                     soft["diag"][:, tb, :], start=True, stop=True)
+                    nc.tensor.transpose(dest[:, col : col + P], soft["e"][:, tb, kb * P : (kb + 1) * P], ident[:])
             a_t = head.tile([P, AT_COLS], BF16, name="a_t")
             nc.vector.tensor_copy(a_t[:, :AT_SPLIT], at_lo[:])
             nc.vector.tensor_copy(a_t[:, AT_SPLIT:], at_hi[:])

@@ -37,13 +37,14 @@ def tile_main_b_kernel(tc, tok_emb, pos_emb, wq, bq, wk, wv, bv, wo, bo, offs, o
     with (
         tc.tile_pool(name="held", bufs=1) as held,
         tc.tile_pool(name="head", bufs=2) as head,
-        tc.tile_pool(name="stage", bufs=3) as stage,
+        tc.tile_pool(name="stage", bufs=6) as stage,
         tc.psum_pool(name="psum", bufs=8) as psum,
     ):
         offsets = held.tile([P, N // 16], U16, name="offsets")
         nc.sync.dma_start(offsets[:], offs)
         tok = [held.tile([P, S], F32, name=f"tok{cb}") for cb in range(CB)]
         pos = [held.tile([P, T], F32, name=f"pos{cb}") for cb in range(CB)]
+        pos_late = [held.tile([P, T], F32, name=f"pos_late{cb}") for cb in range(CB)]
         wq_sb = held.tile([P, CB, C], BF16, name="wq_sb")
         wk_sb = held.tile([P, CB, C], BF16, name="wk_sb")
         wv_sb = held.tile([P, CB, C], BF16, name="wv_sb")
@@ -56,7 +57,7 @@ def tile_main_b_kernel(tc, tok_emb, pos_emb, wq, bq, wk, wv, bv, wo, bo, offs, o
             nc.sync.dma_start(tok[cb][:], tok_emb[rows, :])
             nc.scalar.dma_start(pos[cb][:], pos_emb[rows, :])
             nc.sync.dma_start(wq_sb[:, cb, :], wq[rows, :])
-            nc.scalar.dma_start(wk_sb[:, cb, :], wk[rows, :])
+            nc.sync.dma_start(wk_sb[:, cb, :], wk[rows, :])
         with nc.allow_non_contiguous_dma(reason="one bias value to a partition"):
             nc.sync.dma_start(bq_sb[:], bq.rearrange("(a p) o -> p (a o)", p=P))
         nc.sync.dma_start(wv_sb[:], wv.rearrange("(cb p) m -> p cb m", p=P))
@@ -64,6 +65,8 @@ def tile_main_b_kernel(tc, tok_emb, pos_emb, wq, bq, wk, wv, bv, wo, bo, offs, o
         with nc.allow_non_contiguous_dma(reason="one bias value to a partition"):
             nc.sync.dma_start(bv_sb[:], bv.rearrange("(a p) o -> p (a o)", p=P))
             nc.sync.dma_start(bo_sb[:], bo.rearrange("(a p) o -> p (a o)", p=P))
+        for cb in range(CB):
+            nc.sync.dma_start(pos_late[cb][:], pos_emb[cb * P : (cb + 1) * P, :])
 
         ident = held.tile([P, P], BF16, name="ident")
         make_identity(nc, ident[:])
@@ -73,6 +76,9 @@ def tile_main_b_kernel(tc, tok_emb, pos_emb, wq, bq, wk, wv, bv, wo, bo, offs, o
             out=causal[:], in_=causal[:], pattern=[[-1, P]], compare_op=IS_GE,
             fill=MASKED, base=0, channel_multiplier=1,
         )
+
+        warm = held.tile([P, 1], F32, name="warm")
+        nc.scalar.activation(warm[:], ident[:, 0:1], EXP)
 
         x32 = held.tile([P, CB, N], F32, name="x32")
         xbf = held.tile([P, CB, N], BF16, name="xbf")
@@ -84,11 +90,18 @@ def tile_main_b_kernel(tc, tok_emb, pos_emb, wq, bq, wk, wv, bv, wo, bo, offs, o
         def bank(name, columns=T, dtype=F32):
             return psum.tile([P, columns], dtype, name=name, tag="bank")
 
+        def gather(r, cb, first, count):
+            piece = offsets[:, (r * T + first) // 16 : (r * T + first + count) // 16]
+            pos_cb = pos[cb] if r < 2 else pos_late[cb]
+            nc.vector.tensor_tensor(x32[:, cb, r * T + first : r * T + first + count], tok[cb][:].indirect(piece),
+                                    pos_cb[:, first : first + count], ADD)
+
+        def cast(r, cb):
+            nc.scalar.copy(xbf[:, cb, r * T : (r + 1) * T], x32[:, cb, r * T : (r + 1) * T])
+
         def embed(r, cb):
-            cols = slice(r * T, (r + 1) * T)
-            piece = offsets[:, r * (T // 16) : (r + 1) * (T // 16)]
-            nc.vector.tensor_tensor(x32[:, cb, cols], tok[cb][:].indirect(piece), pos[cb][:], ADD)
-            nc.scalar.copy(xbf[:, cb, cols], x32[:, cb, cols])
+            gather(r, cb, 0, T)
+            cast(r, cb)
 
         def q_part(acc, r, h, cb):
             nc.tensor.matmul(acc[:], wq_sb[:, cb, h * P : (h + 1) * P], xbf[:, cb, r * T : (r + 1) * T],
@@ -103,6 +116,9 @@ def tile_main_b_kernel(tc, tok_emb, pos_emb, wq, bq, wk, wv, bv, wo, bo, offs, o
 
         def k_store(acc, r, h):
             nc.vector.tensor_scalar(out=k[:, h, r * T : (r + 1) * T], in0=acc[:], scalar1=SCALE, scalar2=None, op0=MULT)
+
+        def k_store_on_scalar(acc, r, h):
+            nc.scalar.mul(k[:, h, r * T : (r + 1) * T], acc[:], SCALE)
 
         def v_part(acc, r, tb, cb):
             first = r * T + tb * P
@@ -184,39 +200,56 @@ def tile_main_b_kernel(tc, tok_emb, pos_emb, wq, bq, wk, wv, bv, wo, bo, offs, o
                 q_part(accs_q[h], 0, h, cb)
                 k_part(accs_k[h], 0, h, cb)
             embed(1, cb)
-        soft_next = new_head()
+        for r in range(2, B):
+            for cb in range(CB):
+                gather(r, cb, 0, T)
         for h in range(CB):
             q_store(accs_q[h], 0, h)
-            k_store(accs_k[h], 0, h)
-            if h == 1:
-                for tb in range(TB):
-                    score_block(0, 0, tb, soft_next)
+            k_store_on_scalar(accs_k[h], 0, h)
         for tb in range(TB):
             project(v_part, v_store, 0, tb)
+        project(q_part, q_store, 1, 0)
+        project(k_part, k_store_on_scalar, 1, 0)
+        project(v_part, v_store, 1, 0)
+        soft_next = new_head()
+        for tb in range(TB):
+            score_block(0, 0, tb, soft_next)
         normalisers(soft_next)
+
+        wide = []
+        for m in range(CB + 1, STEPS):
+            wide.extend([(q_part, q_store, m // CB, m % CB), (k_part, k_store, m // CB, m % CB),
+                         (v_part, v_store, m // CB, m % CB)])
+        wide.extend([(out_part, out_store, r, mb) for r in range(B - 1) for mb in range(CB)])
+        IN_A_STEP = len(wide) // (STEPS - 1)
+        casts = [(r, cb) for r in range(2, B) for cb in range(CB)]
 
         for n in range(STEPS):
             r, h = divmod(n, CB)
             soft = soft_next
-            r1, h1 = divmod(n + 1, CB)
-            r2, h2 = divmod(n + 2, CB)
             if n + 1 < STEPS:
                 soft_next = new_head()
                 for tb in range(TB):
-                    score_block(r1, h1, tb, soft_next)
-            if r + 2 < B:
-                embed(r + 2, h)
-            if CB <= n + 2 < STEPS:
-                project(q_part, q_store, r2, h2)
-            a_t = transpose_weights(soft)
-            if CB <= n + 2 < STEPS:
-                project(k_part, k_store, r2, h2)
-            if r + 1 < B:
-                project(v_part, v_store, r + 1, h)
+                    score_block((n + 1) // CB, (n + 1) % CB, tb, soft_next)
+            for later_r, later_cb in casts[2 * n : 2 * n + 2]:
+                cast(later_r, later_cb)
+            if n + 1 < STEPS:
+                groups = wide[IN_A_STEP * n : IN_A_STEP * (n + 1)]
+                project(*groups[0])
+                a_t = transpose_weights(soft)
+                for group in groups[1:]:
+                    project(*group)
+            else:
+                a_t = transpose_weights(soft)
+                accs_out = [bank(f"acc_out{mb}") for mb in range(CB)]
+                for cb in range(CB - 2):
+                    for mb in range(CB):
+                        out_part(accs_out[mb], B - 1, mb, cb)
             weighted_sum(r, h, a_t)
             if n + 1 < STEPS:
                 normalisers(soft_next)
-            if r >= 1:
-                project(out_part, out_store, r - 1, h)
         for mb in range(CB):
-            project(out_part, out_store, B - 1, mb)
+            out_part(accs_out[mb], B - 1, mb, CB - 2)
+        for mb in range(CB):
+            out_part(accs_out[mb], B - 1, mb, CB - 1)
+            out_store(accs_out[mb], B - 1, mb)

@@ -208,12 +208,12 @@ def tile_main_b_kernel(tc, tok_emb, pos_emb, wq, bq, wk, wv, bv, wo, bo, offs, o
             k_store_on_scalar(accs_k[h], 0, h)
         for tb in range(TB):
             project(v_part, v_store, 0, tb)
-        project(q_part, q_store, 1, 0)
-        project(k_part, k_store_on_scalar, 1, 0)
-        project(v_part, v_store, 1, 0)
         soft_next = new_head()
         for tb in range(TB):
             score_block(0, 0, tb, soft_next)
+        project(q_part, q_store, 1, 0)
+        project(k_part, k_store_on_scalar, 1, 0)
+        project(v_part, v_store, 1, 0)
         normalisers(soft_next)
 
         wide = []

@@ -41,7 +41,6 @@ def tile_main_b_kernel(tc, tok_emb, pos_emb, wq, bq, wk, wv, bv, wo, bo, offs, o
         tc.psum_pool(name="psum", bufs=8) as psum,
     ):
         offsets = held.tile([P, N // 16], U16, name="offsets")
-        nc.sync.dma_start(offsets[:], offs)
         tok = [held.tile([P, S], F32, name=f"tok{cb}") for cb in range(CB)]
         pos = [held.tile([P, T], F32, name=f"pos{cb}") for cb in range(CB)]
         pos_late = [held.tile([P, T], F32, name=f"pos_late{cb}") for cb in range(CB)]
@@ -56,17 +55,19 @@ def tile_main_b_kernel(tc, tok_emb, pos_emb, wq, bq, wk, wv, bv, wo, bo, offs, o
             rows = slice(cb * P, (cb + 1) * P)
             nc.sync.dma_start(tok[cb][:], tok_emb[rows, :])
             nc.scalar.dma_start(pos[cb][:], pos_emb[rows, :])
+            if cb == 0:
+                nc.sync.dma_start(offsets[:], offs)
             nc.sync.dma_start(wq_sb[:, cb, :], wq[rows, :])
             nc.sync.dma_start(wk_sb[:, cb, :], wk[rows, :])
         with nc.allow_non_contiguous_dma(reason="one bias value to a partition"):
             nc.sync.dma_start(bq_sb[:], bq.rearrange("(a p) o -> p (a o)", p=P))
         nc.sync.dma_start(wv_sb[:], wv.rearrange("(cb p) m -> p cb m", p=P))
+        for cb in range(CB):
+            nc.sync.dma_start(pos_late[cb][:], pos_emb[cb * P : (cb + 1) * P, :])
         nc.sync.dma_start(wo_sb[:], wo.rearrange("(cb p) m -> p cb m", p=P))
         with nc.allow_non_contiguous_dma(reason="one bias value to a partition"):
             nc.sync.dma_start(bv_sb[:], bv.rearrange("(a p) o -> p (a o)", p=P))
             nc.sync.dma_start(bo_sb[:], bo.rearrange("(a p) o -> p (a o)", p=P))
-        for cb in range(CB):
-            nc.sync.dma_start(pos_late[cb][:], pos_emb[cb * P : (cb + 1) * P, :])
 
         ident = held.tile([P, P], BF16, name="ident")
         make_identity(nc, ident[:])

@@ -170,7 +170,7 @@ def tile_main_b_kernel(tc, tok_emb, pos_emb, wq, bq, wk, wv, bv, wo, bo, offs, o
                 nc.vector.tensor_scalar(out=soft["e"][:, tb, :width], in0=soft["e"][:, tb, :width],
                                         scalar1=soft["inv_sum"][:, tb : tb + 1], scalar2=None, op0=MULT)
 
-        def transpose_weights(soft):
+        def transpose_weights(soft, copy):
             at_lo = bank("at_lo", AT_SPLIT, BF16)
             at_hi = bank("at_hi", AT_COLS - AT_SPLIT, BF16)
             for tb in range(TB):
@@ -179,8 +179,8 @@ def tile_main_b_kernel(tc, tok_emb, pos_emb, wq, bq, wk, wv, bv, wo, bo, offs, o
                     dest, col = (at_lo, col) if col < AT_SPLIT else (at_hi, col - AT_SPLIT)
                     nc.tensor.transpose(dest[:, col : col + P], soft["e"][:, tb, kb * P : (kb + 1) * P], ident[:])
             a_t = head.tile([P, AT_COLS], BF16, name="a_t")
-            nc.vector.tensor_copy(a_t[:, :AT_SPLIT], at_lo[:])
-            nc.vector.tensor_copy(a_t[:, AT_SPLIT:], at_hi[:])
+            copy(a_t[:, :AT_SPLIT], at_lo[:])
+            copy(a_t[:, AT_SPLIT:], at_hi[:])
             return a_t
 
         def weighted_sum(r, h, a_t):
@@ -237,11 +237,11 @@ def tile_main_b_kernel(tc, tok_emb, pos_emb, wq, bq, wk, wv, bv, wo, bo, offs, o
             if n + 1 < STEPS:
                 groups = wide[IN_A_STEP * n : IN_A_STEP * (n + 1)]
                 project(*groups[0])
-                a_t = transpose_weights(soft)
+                a_t = transpose_weights(soft, nc.scalar.copy if groups[0][0] is out_part else nc.vector.tensor_copy)
                 for group in groups[1:]:
                     project(*group)
             else:
-                a_t = transpose_weights(soft)
+                a_t = transpose_weights(soft, nc.scalar.copy)
                 accs_out = [bank(f"acc_out{mb}") for mb in range(CB)]
                 for cb in range(CB - 2):
                     for mb in range(CB):

@@ -30,6 +30,7 @@ AT_WIDTH = [T - kb * P for kb in range(TB)]
 AT_START = [sum(AT_WIDTH[:kb]) for kb in range(TB)]
 AT_COLS = sum(AT_WIDTH)
 AT_SPLIT = AT_START[2]
+BLOCKS = [(tb, kb) for kb in range(TB) for tb in range(kb, TB)]
 
 
 def tile_main_b_kernel(tc, tok_emb, pos_emb, wq, bq, wk, wv, bv, wo, bo, offs, out):
@@ -170,14 +171,19 @@ def tile_main_b_kernel(tc, tok_emb, pos_emb, wq, bq, wk, wv, bv, wo, bo, offs, o
                 nc.vector.tensor_scalar(out=soft["e"][:, tb, :width], in0=soft["e"][:, tb, :width],
                                         scalar1=soft["inv_sum"][:, tb : tb + 1], scalar2=None, op0=MULT)
 
-        def transpose_weights(soft, copy):
+        def transpose_weights(soft, copy, parts):
             at_lo = bank("at_lo", AT_SPLIT, BF16)
             at_hi = bank("at_hi", AT_COLS - AT_SPLIT, BF16)
-            for tb in range(TB):
-                for kb in range(tb + 1):
-                    col = AT_START[kb] + (tb - kb) * P
-                    dest, col = (at_lo, col) if col < AT_SPLIT else (at_hi, col - AT_SPLIT)
-                    nc.tensor.transpose(dest[:, col : col + P], soft["e"][:, tb, kb * P : (kb + 1) * P], ident[:])
+            alone = len(BLOCKS) - len(parts)
+            for index, (tb, kb) in enumerate(BLOCKS):
+                col = AT_START[kb] + (tb - kb) * P
+                dest, col = (at_lo, col) if col < AT_SPLIT else (at_hi, col - AT_SPLIT)
+                nc.tensor.transpose(dest[:, col : col + P], soft["e"][:, tb, kb * P : (kb + 1) * P], ident[:])
+                if index >= alone:
+                    part, store, acc, part_r, i, cb = parts[index - alone]
+                    part(acc, part_r, i, cb)
+                    if cb == CB - 1:
+                        store(acc, part_r, i)
             a_t = head.tile([P, AT_COLS], BF16, name="a_t")
             copy(a_t[:, :AT_SPLIT], at_lo[:])
             copy(a_t[:, AT_SPLIT:], at_hi[:])
@@ -236,16 +242,16 @@ def tile_main_b_kernel(tc, tok_emb, pos_emb, wq, bq, wk, wv, bv, wo, bo, offs, o
                 cast(later_r, later_cb)
             if n + 1 < STEPS:
                 groups = wide[IN_A_STEP * n : IN_A_STEP * (n + 1)]
-                project(*groups[0])
-                a_t = transpose_weights(soft, nc.scalar.copy if groups[0][0] is out_part else nc.vector.tensor_copy)
-                for group in groups[1:]:
-                    project(*group)
+                parts = []
+                for part, store, group_r, i in groups[:2]:
+                    acc = bank("acc")
+                    parts.extend([(part, store, acc, group_r, i, cb) for cb in range(CB)])
+                a_t = transpose_weights(soft, nc.scalar.copy if groups[0][0] is out_part else nc.vector.tensor_copy, parts)
+                project(*groups[2])
             else:
-                a_t = transpose_weights(soft, nc.scalar.copy)
                 accs_out = [bank(f"acc_out{mb}") for mb in range(CB)]
-                for cb in range(CB - 2):
-                    for mb in range(CB):
-                        out_part(accs_out[mb], B - 1, mb, cb)
+                parts = [(out_part, out_store, accs_out[mb], B - 1, mb, cb) for cb in range(CB - 2) for mb in range(CB)]
+                a_t = transpose_weights(soft, nc.scalar.copy, parts)
             weighted_sum(r, h, a_t)
             if n + 1 < STEPS:
                 normalisers(soft_next)

@@ -172,21 +172,23 @@ def tile_main_b_kernel(tc, tok_emb, pos_emb, wq, bq, wk, wv, bv, wo, bo, offs, o
                                         scalar1=soft["inv_sum"][:, tb : tb + 1], scalar2=None, op0=MULT)
 
         def transpose_weights(soft, copy, parts):
-            at_lo = bank("at_lo", AT_SPLIT, BF16)
-            at_hi = bank("at_hi", AT_COLS - AT_SPLIT, BF16)
+            a_t = head.tile([P, AT_COLS], BF16, name="a_t")
+            banks = [bank("at_lo", AT_SPLIT, BF16), bank("at_hi", AT_COLS - AT_SPLIT, BF16)]
             alone = len(BLOCKS) - len(parts)
             for index, (tb, kb) in enumerate(BLOCKS):
-                col = AT_START[kb] + (tb - kb) * P
-                dest, col = (at_lo, col) if col < AT_SPLIT else (at_hi, col - AT_SPLIT)
-                nc.tensor.transpose(dest[:, col : col + P], soft["e"][:, tb, kb * P : (kb + 1) * P], ident[:])
+                half = kb // 2
+                col = AT_START[kb] + (tb - kb) * P - half * AT_SPLIT
+                nc.tensor.transpose(banks[half][:, col : col + P], soft["e"][:, tb, kb * P : (kb + 1) * P], ident[:])
+                if tb == TB - 1 and kb % 2 == 1:
+                    if half == 0:
+                        copy(a_t[:, :AT_SPLIT], banks[half][:])
+                    else:
+                        copy(a_t[:, AT_SPLIT:], banks[half][:])
                 if index >= alone:
                     part, store, acc, part_r, i, cb = parts[index - alone]
                     part(acc, part_r, i, cb)
                     if cb == CB - 1:
                         store(acc, part_r, i)
-            a_t = head.tile([P, AT_COLS], BF16, name="a_t")
-            copy(a_t[:, :AT_SPLIT], at_lo[:])
-            copy(a_t[:, AT_SPLIT:], at_hi[:])
             return a_t
 
         def weighted_sum(r, h, a_t):
@@ -240,6 +242,8 @@ def tile_main_b_kernel(tc, tok_emb, pos_emb, wq, bq, wk, wv, bv, wo, bo, offs, o
                     score_block((n + 1) // CB, (n + 1) % CB, tb, soft_next)
             for later_r, later_cb in casts[2 * n : 2 * n + 2]:
                 cast(later_r, later_cb)
+            if n > 0:
+                weighted_sum((n - 1) // CB, (n - 1) % CB, a_t)
             if n + 1 < STEPS:
                 groups = wide[IN_A_STEP * n : IN_A_STEP * (n + 1)]
                 parts = []
@@ -252,9 +256,9 @@ def tile_main_b_kernel(tc, tok_emb, pos_emb, wq, bq, wk, wv, bv, wo, bo, offs, o
                 accs_out = [bank(f"acc_out{mb}") for mb in range(CB)]
                 parts = [(out_part, out_store, accs_out[mb], B - 1, mb, cb) for cb in range(CB - 2) for mb in range(CB)]
                 a_t = transpose_weights(soft, nc.scalar.copy, parts)
-            weighted_sum(r, h, a_t)
             if n + 1 < STEPS:
                 normalisers(soft_next)
+        weighted_sum(B - 1, CB - 1, a_t)
         for mb in range(CB):
             out_part(accs_out[mb], B - 1, mb, CB - 2)
         for mb in range(CB):

@@ -98,23 +98,25 @@ def tile_main_b_kernel(tc, tok_emb, pos_emb, wq, bq, wk, wv, bv, wo, bo, offs, o
             nc.vector.tensor_tensor(x32[:, cb, r * T + first : r * T + first + count], tok[cb][:].indirect(piece),
                                     pos_cb[:, first : first + count], ADD)
 
-        def cast(r, cb):
-            nc.scalar.copy(xbf[:, cb, r * T : (r + 1) * T], x32[:, cb, r * T : (r + 1) * T])
+        def cast(r, cb, first=0, count=T):
+            nc.scalar.copy(xbf[:, cb, r * T + first : r * T + first + count], x32[:, cb, r * T + first : r * T + first + count])
 
         def embed(r, cb):
             gather(r, cb, 0, T)
             cast(r, cb)
 
-        def q_part(acc, r, h, cb):
-            nc.tensor.matmul(acc[:], wq_sb[:, cb, h * P : (h + 1) * P], xbf[:, cb, r * T : (r + 1) * T],
-                             start=(cb == 0), stop=(cb == CB - 1))
+        def q_part(acc, r, h, cb, first=0, count=T):
+            nc.tensor.matmul(acc[:, first : first + count], wq_sb[:, cb, h * P : (h + 1) * P],
+                             xbf[:, cb, r * T + first : r * T + first + count],
+                             start=(cb == 0 and first == 0), stop=(cb == CB - 1))
 
         def q_store(acc, r, h):
             nc.scalar.activation(q[:, h, r * T : (r + 1) * T], acc[:], IDENTITY, bias=bq_sb[:, h : h + 1], scale=1.0)
 
-        def k_part(acc, r, h, cb):
-            nc.tensor.matmul(acc[:], wk_sb[:, cb, h * P : (h + 1) * P], xbf[:, cb, r * T : (r + 1) * T],
-                             start=(cb == 0), stop=(cb == CB - 1))
+        def k_part(acc, r, h, cb, first=0, count=T):
+            nc.tensor.matmul(acc[:, first : first + count], wk_sb[:, cb, h * P : (h + 1) * P],
+                             xbf[:, cb, r * T + first : r * T + first + count],
+                             start=(cb == 0 and first == 0), stop=(cb == CB - 1))
 
         def k_store(acc, r, h):
             nc.vector.tensor_scalar(out=k[:, h, r * T : (r + 1) * T], in0=acc[:], scalar1=SCALE, scalar2=None, op0=MULT)
@@ -204,26 +206,30 @@ def tile_main_b_kernel(tc, tok_emb, pos_emb, wq, bq, wk, wv, bv, wo, bo, offs, o
         accs_q = [bank(f"acc_q{h}") for h in range(CB)]
         accs_k = [bank(f"acc_k{h}") for h in range(CB)]
         for cb in range(CB):
-            embed(0, cb)
-            for h in range(CB):
-                q_part(accs_q[h], 0, h, cb)
-                k_part(accs_k[h], 0, h, cb)
+            count = T // 2 if cb == 0 else T
+            for first in range(0, T, count):
+                gather(0, cb, first, count)
+                cast(0, cb, first, count)
+                for h in range(CB):
+                    q_part(accs_q[h], 0, h, cb, first, count)
+                    k_part(accs_k[h], 0, h, cb, first, count)
             embed(1, cb)
-        for r in range(2, B):
-            for cb in range(CB):
-                gather(r, cb, 0, T)
         for h in range(CB):
             q_store(accs_q[h], 0, h)
             k_store_on_scalar(accs_k[h], 0, h)
-        for tb in range(TB):
-            project(v_part, v_store, 0, tb)
+        project(v_part, v_store, 0, 0)
         soft_next = new_head()
         for tb in range(TB):
             score_block(0, 0, tb, soft_next)
+        for r in range(2, B):
+            for cb in range(CB):
+                gather(r, cb, 0, T)
+        for tb in range(1, TB):
+            project(v_part, v_store, 0, tb)
+        normalisers(soft_next)
         project(q_part, q_store, 1, 0)
         project(k_part, k_store_on_scalar, 1, 0)
         project(v_part, v_store, 1, 0)
-        normalisers(soft_next)
 
         wide = []
         for m in range(CB + 1, STEPS):

@@ -52,14 +52,29 @@ def tile_main_b_kernel(tc, tok_emb, pos_emb, wq, bq, wk, wv, bv, wo, bo, offs, o
         bq_sb = held.tile([P, CB], F32, name="bq_sb")
         bv_sb = held.tile([P, CB], F32, name="bv_sb")
         bo_sb = held.tile([P, CB], F32, name="bo_sb")
-        for cb in range(CB):
-            rows = slice(cb * P, (cb + 1) * P)
-            nc.sync.dma_start(tok[cb][:], tok_emb[rows, :])
-            nc.scalar.dma_start(pos[cb][:], pos_emb[rows, :])
+        def load_x_rows(cb):
+            nc.sync.dma_start(tok[cb][:], tok_emb[cb * P : (cb + 1) * P, :])
             if cb == 0:
                 nc.sync.dma_start(offsets[:], offs)
-            nc.sync.dma_start(wq_sb[:, cb, :], wq[rows, :])
-            nc.sync.dma_start(wk_sb[:, cb, :], wk[rows, :])
+                nc.sync.dma_start(pos[cb][:, : T // 2], pos_emb[cb * P : (cb + 1) * P, : T // 2])
+                nc.sync.dma_start(wq_sb[:, cb, :], wq[cb * P : (cb + 1) * P, :])
+                nc.sync.dma_start(pos[cb][:, T // 2 :], pos_emb[cb * P : (cb + 1) * P, T // 2 :])
+            else:
+                nc.sync.dma_start(pos[cb][:], pos_emb[cb * P : (cb + 1) * P, :])
+
+        def load_weight_rows(cb):
+            if cb > 0:
+                nc.sync.dma_start(wq_sb[:, cb, :], wq[cb * P : (cb + 1) * P, :])
+            nc.sync.dma_start(wk_sb[:, cb, :], wk[cb * P : (cb + 1) * P, :])
+
+        load_x_rows(0)
+        load_weight_rows(0)
+        load_x_rows(1)
+        load_weight_rows(1)
+        load_x_rows(2)
+        load_x_rows(3)
+        load_weight_rows(2)
+        load_weight_rows(3)
         with nc.allow_non_contiguous_dma(reason="one bias value to a partition"):
             nc.sync.dma_start(bq_sb[:], bq.rearrange("(a p) o -> p (a o)", p=P))
         nc.sync.dma_start(wv_sb[:], wv.rearrange("(cb p) m -> p cb m", p=P))
@@ -261,7 +276,7 @@ def tile_main_b_kernel(tc, tok_emb, pos_emb, wq, bq, wk, wv, bv, wo, bo, offs, o
             else:
                 accs_out = [bank(f"acc_out{mb}") for mb in range(CB)]
                 parts = [(out_part, out_store, accs_out[mb], B - 1, mb, cb) for cb in range(CB - 2) for mb in range(CB)]
-                a_t = transpose_weights(soft, nc.scalar.copy, parts)
+                a_t = transpose_weights(soft, nc.vector.tensor_copy, parts)
             if n + 1 < STEPS:
                 normalisers(soft_next)
         weighted_sum(B - 1, CB - 1, a_t)

import math

import concourse.mybir as mybir
from concourse.masks import make_identity

F32 = mybir.dt.float32
BF16 = mybir.dt.bfloat16
U16 = mybir.dt.uint16
ADD = mybir.AluOpType.add
MULT = mybir.AluOpType.mult
IS_GE = mybir.AluOpType.is_ge
EXP = mybir.ActivationFunctionType.Exp
IDENTITY = mybir.ActivationFunctionType.Identity
X_AXIS = mybir.AxisListType.X

P = 128
C = 512
S = 1024
T = 512
B = 4
N = B * T
CB = C // P
TB = T // P
SCALE = 1.0 / math.sqrt(P)
MASKED = -1.0e10

FLOPS = 4 * 2 * C * C * N + B * CB * 2 * 2 * P * (T * (T + 1) // 2)

AT_WIDTH = [T - kb * P for kb in range(TB)]
AT_START = [sum(AT_WIDTH[:kb]) for kb in range(TB)]
AT_COLS = sum(AT_WIDTH)
AT_SPLIT = AT_START[2]
BLOCKS = [(tb, kb) for kb in range(TB) for tb in range(kb, TB)]


def tile_main_b_kernel(tc, tok_emb, pos_emb, wq, bq, wk, wv, bv, wo, bo, offs, out):
    nc = tc.nc
    with (
        tc.tile_pool(name="held", bufs=1) as held,
        tc.tile_pool(name="head", bufs=2) as head,
        tc.tile_pool(name="stage", bufs=6) as stage,
        tc.psum_pool(name="psum", bufs=8) as psum,
    ):
        offsets = held.tile([P, N // 16], U16, name="offsets")
        tok = [held.tile([P, S], F32, name=f"tok{cb}") for cb in range(CB)]
        pos = [held.tile([P, T], F32, name=f"pos{cb}") for cb in range(CB)]
        pos_late = [held.tile([P, T], F32, name=f"pos_late{cb}") for cb in range(CB)]
        wq_sb = held.tile([P, CB, C], BF16, name="wq_sb")
        wk_sb = held.tile([P, CB, C], BF16, name="wk_sb")
        wv_sb = held.tile([P, CB, C], BF16, name="wv_sb")
        wo_sb = held.tile([P, CB, C], BF16, name="wo_sb")
        bq_sb = held.tile([P, CB], F32, name="bq_sb")
        bv_sb = held.tile([P, CB], F32, name="bv_sb")
        bo_sb = held.tile([P, CB], F32, name="bo_sb")
        def load_x_rows(cb):
            nc.sync.dma_start(tok[cb][:], tok_emb[cb * P : (cb + 1) * P, :])
            if cb == 0:
                nc.sync.dma_start(offsets[:], offs)
                nc.sync.dma_start(pos[cb][:, : T // 2], pos_emb[cb * P : (cb + 1) * P, : T // 2])
                nc.sync.dma_start(wq_sb[:, cb, :], wq[cb * P : (cb + 1) * P, :])
                nc.sync.dma_start(pos[cb][:, T // 2 :], pos_emb[cb * P : (cb + 1) * P, T // 2 :])
            else:
                nc.sync.dma_start(pos[cb][:], pos_emb[cb * P : (cb + 1) * P, :])

        def load_weight_rows(cb):
            if cb > 0:
                nc.sync.dma_start(wq_sb[:, cb, :], wq[cb * P : (cb + 1) * P, :])
            nc.sync.dma_start(wk_sb[:, cb, :], wk[cb * P : (cb + 1) * P, :])

        load_x_rows(0)
        load_weight_rows(0)
        load_x_rows(1)
        load_weight_rows(1)
        load_x_rows(2)
        load_x_rows(3)
        load_weight_rows(2)
        load_weight_rows(3)
        with nc.allow_non_contiguous_dma(reason="one bias value to a partition"):
            nc.sync.dma_start(bq_sb[:], bq.rearrange("(a p) o -> p (a o)", p=P))
        nc.sync.dma_start(wv_sb[:], wv.rearrange("(cb p) m -> p cb m", p=P))
        for cb in range(CB):
            nc.sync.dma_start(pos_late[cb][:], pos_emb[cb * P : (cb + 1) * P, :])
        nc.sync.dma_start(wo_sb[:], wo.rearrange("(cb p) m -> p cb m", p=P))
        with nc.allow_non_contiguous_dma(reason="one bias value to a partition"):
            nc.sync.dma_start(bv_sb[:], bv.rearrange("(a p) o -> p (a o)", p=P))
            nc.sync.dma_start(bo_sb[:], bo.rearrange("(a p) o -> p (a o)", p=P))

        ident = held.tile([P, P], BF16, name="ident")
        make_identity(nc, ident[:])
        causal = held.tile([P, P], BF16, name="causal")
        nc.gpsimd.memset(causal[:], 0.0)
        nc.gpsimd.affine_select(
            out=causal[:], in_=causal[:], pattern=[[-1, P]], compare_op=IS_GE,
            fill=MASKED, base=0, channel_multiplier=1,
        )

        warm = held.tile([P, 1], F32, name="warm")
        nc.scalar.activation(warm[:], ident[:, 0:1], EXP)

        x32 = held.tile([P, CB, N], F32, name="x32")
        xbf = held.tile([P, CB, N], BF16, name="xbf")
        q = held.tile([P, CB, N], BF16, name="q")
        k = held.tile([P, CB, N], BF16, name="k")
        v_t = held.tile([P, B * TB, C], BF16, name="v_t")
        o = held.tile([P, CB, N], BF16, name="o")

        def bank(name, columns=T, dtype=F32):
            return psum.tile([P, columns], dtype, name=name, tag="bank")

        def gather(r, cb, first, count):
            piece = offsets[:, (r * T + first) // 16 : (r * T + first + count) // 16]
            pos_cb = pos[cb] if r < 2 else pos_late[cb]
            nc.vector.tensor_tensor(x32[:, cb, r * T + first : r * T + first + count], tok[cb][:].indirect(piece),
                                    pos_cb[:, first : first + count], ADD)

        def cast(r, cb, first=0, count=T):
            nc.scalar.copy(xbf[:, cb, r * T + first : r * T + first + count], x32[:, cb, r * T + first : r * T + first + count])

        def embed(r, cb):
            gather(r, cb, 0, T)
            cast(r, cb)

        def q_part(acc, r, h, cb, first=0, count=T):
            nc.tensor.matmul(acc[:, first : first + count], wq_sb[:, cb, h * P : (h + 1) * P],
                             xbf[:, cb, r * T + first : r * T + first + count],
                             start=(cb == 0 and first == 0), stop=(cb == CB - 1))

        def q_store(acc, r, h):
            nc.scalar.activation(q[:, h, r * T : (r + 1) * T], acc[:], IDENTITY, bias=bq_sb[:, h : h + 1], scale=1.0)

        def k_part(acc, r, h, cb, first=0, count=T):
            nc.tensor.matmul(acc[:, first : first + count], wk_sb[:, cb, h * P : (h + 1) * P],
                             xbf[:, cb, r * T + first : r * T + first + count],
                             start=(cb == 0 and first == 0), stop=(cb == CB - 1))

        def k_store(acc, r, h):
            nc.vector.tensor_scalar(out=k[:, h, r * T : (r + 1) * T], in0=acc[:], scalar1=SCALE, scalar2=None, op0=MULT)

        def k_store_on_scalar(acc, r, h):
            nc.scalar.mul(k[:, h, r * T : (r + 1) * T], acc[:], SCALE)

        def v_part(acc, r, tb, cb):
            first = r * T + tb * P
            nc.tensor.matmul(acc[:], xbf[:, cb, first : first + P], wv_sb[:, cb, :],
                             start=(cb == 0), stop=(cb == CB - 1))

        def v_store(acc, r, tb):
            nc.scalar.copy(v_t[:, r * TB + tb, :], acc[:])

        def out_part(acc, r, mb, cb):
            nc.tensor.matmul(acc[:], wo_sb[:, cb, mb * P : (mb + 1) * P], o[:, cb, r * T : (r + 1) * T],
                             start=(cb == 0), stop=(cb == CB - 1))

        def out_store(acc, r, mb):
            res = stage.tile([P, T], F32, name="res")
            nc.vector.scalar_tensor_tensor(out=res[:], in0=acc[:], scalar=bo_sb[:, mb : mb + 1],
                                           in1=x32[:, mb, r * T : (r + 1) * T], op0=ADD, op1=ADD)
            nc.sync.dma_start(out[mb * P : (mb + 1) * P, r * T : (r + 1) * T], res[:])

        def project(part, store, r, i):
            acc = bank("acc")
            for cb in range(CB):
                part(acc, r, i, cb)
            store(acc, r, i)

        def new_head():
            return {
                "neg_max": head.tile([P, TB], F32, name="neg_max"),
                "row_sum": head.tile([P, TB], F32, name="row_sum"),
                "inv_sum": head.tile([P, TB], F32, name="inv_sum"),
                "e": head.tile([P, TB, T], BF16, name="e"),
            }

        def score_block(r, h, tb, soft):
            width = (tb + 1) * P
            score = bank("score")
            nc.tensor.matmul(score[:, :width], q[:, h, r * T + tb * P : r * T + width], k[:, h, r * T : r * T + width],
                             start=True, stop=False)
            nc.tensor.matmul(score[:, tb * P : width], ident[:], causal[:], start=False, stop=True)
            nc.vector.reduce_max(soft["neg_max"][:, tb : tb + 1], score[:, :width], X_AXIS, negate=True)
            nc.scalar.activation(soft["e"][:, tb, :width], score[:, :width], EXP, bias=soft["neg_max"][:, tb : tb + 1],
                                 scale=1.0, accum_out=soft["row_sum"][:, tb : tb + 1])

        def normalisers(soft):
            nc.vector.reciprocal(soft["inv_sum"][:], soft["row_sum"][:])
            for tb in range(TB):
                width = (tb + 1) * P
                nc.vector.tensor_scalar(out=soft["e"][:, tb, :width], in0=soft["e"][:, tb, :width],
                                        scalar1=soft["inv_sum"][:, tb : tb + 1], scalar2=None, op0=MULT)

        def transpose_weights(soft, copy, parts):
            a_t = head.tile([P, AT_COLS], BF16, name="a_t")
            banks = [bank("at_lo", AT_SPLIT, BF16), bank("at_hi", AT_COLS - AT_SPLIT, BF16)]
            alone = len(BLOCKS) - len(parts)
            for index, (tb, kb) in enumerate(BLOCKS):
                half = kb // 2
                col = AT_START[kb] + (tb - kb) * P - half * AT_SPLIT
                nc.tensor.transpose(banks[half][:, col : col + P], soft["e"][:, tb, kb * P : (kb + 1) * P], ident[:])
                if tb == TB - 1 and kb % 2 == 1:
                    if half == 0:
                        copy(a_t[:, :AT_SPLIT], banks[half][:])
                    else:
                        copy(a_t[:, AT_SPLIT:], banks[half][:])
                if index >= alone:
                    part, store, acc, part_r, i, cb = parts[index - alone]
                    part(acc, part_r, i, cb)
                    if cb == CB - 1:
                        store(acc, part_r, i)
            return a_t

        def weighted_sum(r, h, a_t):
            o_acc = bank("o_acc")
            for kb in range(TB):
                nc.tensor.matmul(o_acc[:, kb * P :], v_t[:, r * TB + kb, h * P : (h + 1) * P],
                                 a_t[:, AT_START[kb] : AT_START[kb] + AT_WIDTH[kb]],
                                 start=(kb == 0), stop=(kb == TB - 1))
            nc.scalar.activation(o[:, h, r * T : (r + 1) * T], o_acc[:], IDENTITY, bias=bv_sb[:, h : h + 1], scale=1.0)

        STEPS = B * CB

        accs_q = [bank(f"acc_q{h}") for h in range(CB)]
        accs_k = [bank(f"acc_k{h}") for h in range(CB)]
        for cb in range(CB):
            count = T // 2 if cb == 0 else T
            for first in range(0, T, count):
                gather(0, cb, first, count)
                cast(0, cb, first, count)
                for h in range(CB):
                    q_part(accs_q[h], 0, h, cb, first, count)
                    k_part(accs_k[h], 0, h, cb, first, count)
            embed(1, cb)
        for h in range(CB):
            q_store(accs_q[h], 0, h)
            k_store_on_scalar(accs_k[h], 0, h)
        project(v_part, v_store, 0, 0)
        soft_next = new_head()
        for tb in range(TB):
            score_block(0, 0, tb, soft_next)
        for r in range(2, B):
            for cb in range(CB):
                gather(r, cb, 0, T)
        for tb in range(1, TB):
            project(v_part, v_store, 0, tb)
        normalisers(soft_next)
        project(q_part, q_store, 1, 0)
        project(k_part, k_store_on_scalar, 1, 0)
        project(v_part, v_store, 1, 0)

        wide = []
        for m in range(CB + 1, STEPS):
            wide.extend([(q_part, q_store, m // CB, m % CB), (k_part, k_store, m // CB, m % CB),
                         (v_part, v_store, m // CB, m % CB)])
        wide.extend([(out_part, out_store, r, mb) for r in range(B - 1) for mb in range(CB)])
        IN_A_STEP = len(wide) // (STEPS - 1)
        casts = [(r, cb) for r in range(2, B) for cb in range(CB)]

        for n in range(STEPS):
            r, h = divmod(n, CB)
            soft = soft_next
            if n + 1 < STEPS:
                soft_next = new_head()
                for tb in range(TB):
                    score_block((n + 1) // CB, (n + 1) % CB, tb, soft_next)
            for later_r, later_cb in casts[2 * n : 2 * n + 2]:
                cast(later_r, later_cb)
            if n > 0:
                weighted_sum((n - 1) // CB, (n - 1) % CB, a_t)
            if n + 1 < STEPS:
                groups = wide[IN_A_STEP * n : IN_A_STEP * (n + 1)]
                parts = []
                for part, store, group_r, i in groups[:2]:
                    acc = bank("acc")
                    parts.extend([(part, store, acc, group_r, i, cb) for cb in range(CB)])
                a_t = transpose_weights(soft, nc.scalar.copy if groups[0][0] is out_part else nc.vector.tensor_copy, parts)
                project(*groups[2])
            else:
                accs_out = [bank(f"acc_out{mb}") for mb in range(CB)]
                parts = [(out_part, out_store, accs_out[mb], B - 1, mb, cb) for cb in range(CB - 2) for mb in range(CB)]
                a_t = transpose_weights(soft, nc.vector.tensor_copy, parts)
            if n + 1 < STEPS:
                normalisers(soft_next)
        weighted_sum(B - 1, CB - 1, a_t)
        for mb in range(CB):
            out_part(accs_out[mb], B - 1, mb, CB - 2)
        for mb in range(CB):
            out_part(accs_out[mb], B - 1, mb, CB - 1)
            out_store(accs_out[mb], B - 1, mb)
